import numpy as np
import ml_dtypes


def mxq(x, axis, fmt="e4m3"):
    dtype, down = {"e4m3": (ml_dtypes.float8_e4m3fn, 7), "e5m2": (ml_dtypes.float8_e5m2, 14)}[fmt]
    v = np.moveaxis(np.asarray(x, np.float32).astype(ml_dtypes.bfloat16).astype(np.float64), axis, -1)
    blocks = v.reshape(v.shape[:-1] + (-1, 32))
    amax = np.abs(blocks).max(-1, keepdims=True)
    byte = np.maximum(np.where(amax > 0, np.frexp(amax)[1] - 1 + 127, 0) - down, 1)
    scale = np.exp2(byte - 127.0)
    codes = (blocks / scale).astype(np.float32).astype(dtype).astype(np.float64)
    return np.moveaxis((codes * scale).reshape(v.shape), -1, axis)


WIDE = False


def mx_kscale(k):
    if not WIDE:
        return np.ones(k)
    levels = np.array([10, -10, 5, -5, 0])
    a = np.random.permutation(np.resize(levels, k // 512 * 4)).reshape(k // 512, 4)
    idx = np.arange(k)
    return np.exp2(a[idx // 512, idx % 128 // 32])


BF16 = ml_dtypes.bfloat16


def bf(x):
    return np.asarray(x, np.float32).astype(BF16)


def f64(x):
    return np.asarray(x).astype(np.float64)


B, C, E, H, HS, WS = 2, 512, 1536, 16, 32, 32
N = HS * WS
EPS = 1e-5
A = 2.0 * (E / H) ** -0.5 / np.sqrt(N)


def chan_layernorm(x, g):
    mean = x.mean(axis=1, keepdims=True)
    var = x.var(axis=1, keepdims=True)
    return (x - mean) * (1.0 / np.sqrt(var + EPS)) * g


def setup_inputs():
    s = mx_kscale(E)
    return {"h_attn": bf(np.random.standard_normal((B, E, HS, WS)) * A * s[None, :, None, None]),
            "xn": bf(np.random.standard_normal((B, C, HS, WS))),
            "Wout": bf(np.random.standard_normal((C, E)) / (np.sqrt(E) * A) / s[None, :]),
            "bout": bf(0.3 * np.random.standard_normal(C)),
            "outnorm_g": bf(1.0 + 0.1 * np.random.standard_normal((1, C, 1, 1)))}


def reference(h_attn, xn, Wout, bout, outnorm_g):
    a = f64(h_attn).reshape(B, E, N)
    y = (mxq(f64(Wout), 1, "e4m3") @ mxq(a, 1, "e4m3")) + f64(bout)[None, :, None]
    y = y.reshape(B, C, HS, WS)
    return chan_layernorm(y, f64(outnorm_g)) + f64(xn)

@@ -1,0 +1,261 @@
+from contextlib import ExitStack
+
+import concourse.mybir as mybir
+from concourse.masks import make_identity
+
+F32 = mybir.dt.float32
+BF16 = mybir.dt.bfloat16
+U32 = mybir.dt.uint32
+U8 = mybir.dt.uint8
+FP8X4 = mybir.dt.float8_e4m3fn_x4
+ALU = mybir.AluOpType
+ACT = mybir.ActivationFunctionType
+
+P = 128
+PACK = 4
+K_PASS = P * PACK
+IMAGES, C, E, N = 2, 512, 1536, 1024
+PASSES = E // K_PASS
+C_TILES = C // P
+GROUP = 512
+TILES = GROUP // P
+HALVES = N // GROUP
+ALL_TILES = IMAGES * N // P
+EPS = 1e-5
+VECTOR_POSITIONS = 512
+LEAD = 3
+LAG = 7
+
+FLOPS = 2 * IMAGES * N * C * E
+
+
+def tile_linearattention_pb_kernel(tc, h_attn, xn, Wout, bout, outnorm_g, out):
+    nc = tc.nc
+    h_rows = h_attn.rearrange("b e y x -> b e (y x)")
+    xn_rows = xn.rearrange("b (p t) y x -> b p t (y x)", t=C_TILES)
+    out_rows = out.rearrange("b (p t) y x -> b p t (y x)", t=C_TILES)
+    w_rows = Wout.rearrange("(p t) e -> p t e", t=C_TILES)
+
+    with ExitStack() as ctx:
+        keep = ctx.enter_context(tc.tile_pool(name="keep", bufs=1))
+        stage = ctx.enter_context(tc.tile_pool(name="stage", bufs=3))
+        work = ctx.enter_context(tc.tile_pool(name="work", bufs=4))
+        stats = ctx.enter_context(tc.tile_pool(name="stats", bufs=4))
+        psum = ctx.enter_context(tc.psum_pool(name="psum", bufs=4))
+        ctx.enter_context(tc.manual_schedule())
+
+        bias_row = keep.tile([P, C], BF16)
+        nc.vector.memset(bias_row[:], 0.0)
+        nc.scalar.dma_start(out=bias_row[0:1, :], in_=bout.rearrange("(o c) -> o c", o=1))
+        gain_bf = keep.tile([P, C_TILES], BF16)
+        with nc.allow_non_contiguous_dma(reason="four gains to a partition"):
+            nc.scalar.dma_start(
+                out=gain_bf[:],
+                in_=outnorm_g.rearrange("o c y x -> (o c y x)").rearrange("(p t) -> p t", t=C_TILES),
+            )
+
+        h_raw = {}
+        for b in range(IMAGES):
+            for g in range(PASSES):
+                h_raw[(b, g)] = keep.tile([P, PACK, N], BF16, name="h_raw_%d_%d" % (b, g))
+
+        def load_h(b, g):
+            nc.sync.dma_start(
+                out=h_raw[(b, g)][:],
+                in_=h_rows[b, g * K_PASS : (g + 1) * K_PASS, :].rearrange("(p j) w -> p j w", j=PACK),
+            )
+
+        w_raw = keep.tile([P, C_TILES, E], BF16)
+        load_h(0, 0)
+        nc.sync.dma_start(out=w_raw[:], in_=w_rows)
+        load_h(0, 1)
+        load_h(0, 2)
+        for g in range(PASSES):
+            load_h(1, g)
+        xn_sb = []
+        for b in range(IMAGES):
+            xn_b = keep.tile([P, C_TILES, N], BF16, name="xn_%d" % b)
+            nc.sync.dma_start(out=xn_b[:], in_=xn_rows[b])
+            xn_sb.append(xn_b)
+
+        ident = keep.tile([P, P], F32)
+        make_identity(nc, ident[:])
+        ones = keep.tile([P, P], BF16)
+        nc.vector.memset(ones[:], 1.0)
+        one_col = keep.tile([P, 1], F32)
+        nc.vector.memset(one_col[:], 1.0)
+        warm_col = keep.tile([P, 1], F32)
+        nc.scalar.activation(out=warm_col[:], in_=one_col[:], func=ACT.Abs_reciprocal_sqrt)
+
+        h_codes = {}
+        h_scales = {}
+
+        def regroup(b, g):
+            raw = h_raw[(b, g)]
+            grouped = stage.tile([P, N, PACK], BF16, align_bytes=64, name="grouped")
+            split = VECTOR_POSITIONS
+            nc.vector.tensor_copy(
+                out=grouped[:, 0:split, :].rearrange("p (c i) t -> p c t i", i=4),
+                in_=raw[:, :, 0:split].rearrange("p t (c i) -> p c t i", i=4),
+            )
+            nc.scalar.copy(
+                out=grouped[:, split:N, :].rearrange("p (c i) t -> p c t i", i=4),
+                in_=raw[:, :, split:N].rearrange("p t (c i) -> p c t i", i=4),
+            )
+            return grouped
+
+        def quantise(b, g, grouped):
+            codes = keep.tile([P, N], U32, align_bytes=64, name="h_codes_%d_%d" % (b, g))
+            scales = keep.tile([P, N], U8, align_bytes=64, name="h_scales_%d_%d" % (b, g))
+            for half in range(HALVES):
+                cols = slice(half * GROUP, (half + 1) * GROUP)
+                nc.vector.quantize_mx(
+                    out=codes[:, cols].bitcast(FP8X4),
+                    scales=scales[:, cols],
+                    in_=grouped[:, cols, :].rearrange("p w j -> p (w j)"),
+                )
+            h_codes[(b, g)] = codes
+            h_scales[(b, g)] = scales
+
+        chunks = [(b, g) for b in range(IMAGES) for g in range(PASSES)]
+        quantise(0, 0, regroup(0, 0))
+
+        w_words = w_raw[:].bitcast(F32).rearrange("p t (g q u) -> p t g u q", g=PASSES, u=2)
+        w_grouped = keep.tile([P, PASSES, C, PACK], BF16, align_bytes=64)
+        w_grouped_words = w_grouped[:].bitcast(F32)
+        w_codes = keep.tile([P, PASSES, C], U32, align_bytes=64)
+        w_scales = keep.tile([P, PASSES, C], U8, align_bytes=64)
+        for g in range(PASSES):
+            for pair in range(2):
+                turned = psum.tile([P, 2, 2, P], F32, tag="turn")
+                for tt in range(2):
+                    for u in range(2):
+                        nc.tensor.transpose(turned[:, tt, u, :], w_words[:, 2 * pair + tt, g, u, :], ident[:])
+                nc.scalar.copy(
+                    out=w_grouped_words[:, g, 2 * pair * P : (2 * pair + 2) * P, :].rearrange(
+                        "p (tt c) u -> p tt c u", tt=2
+                    ),
+                    in_=turned[:].rearrange("p tt u c -> p tt c u"),
+                )
+            nc.vector.quantize_mx(
+                out=w_codes[:, g, :].bitcast(FP8X4),
+                scales=w_scales[:, g, :],
+                in_=w_grouped[:, g, :, :].rearrange("p c j -> p (c j)"),
+            )
+
+        bias_ps = psum.tile([P, C], F32, tag="turn")
+        nc.tensor.matmul(out=bias_ps[:], lhsT=ones[:], rhs=bias_row[:], start=True, stop=True)
+        bias_all = keep.tile([P, C_TILES, P], F32)
+        nc.vector.tensor_copy(out=bias_all[:], in_=bias_ps[:].rearrange("p (q t) -> p t q", t=C_TILES))
+        gain = keep.tile([P, C_TILES], F32)
+        nc.vector.tensor_copy(out=gain[:], in_=gain_bf[:])
+
+        waiting = regroup(*chunks[1])
+        for c in range(2, len(chunks)):
+            grouped = regroup(*chunks[c])
+            quantise(chunks[c - 1][0], chunks[c - 1][1], waiting)
+            waiting = grouped
+        quantise(chunks[-1][0], chunks[-1][1], waiting)
+
+        z_of = {}
+        y_of = {}
+        neg_mean_of = {}
+        rstd_of = {}
+        normed_of = {}
+
+        def project(n):
+            b, first = n * P // N, n * P % N
+            cols = slice(first, first + P)
+            z = psum.tile([P, C], F32, tag="z")
+            for g in range(PASSES):
+                nc.tensor.matmul_mx(
+                    out=z[:],
+                    lhsT=h_codes[(b, g)][:, cols].bitcast(FP8X4),
+                    lhsT_scale=h_scales[(b, g)][:, cols],
+                    rhs=w_codes[:, g, :].bitcast(FP8X4),
+                    rhs_scale=w_scales[:, g, :],
+                    start=(g == 0),
+                    stop=(g == PASSES - 1),
+                )
+            z_of[n] = z
+
+        def add_bias_and_measure(n):
+            y = work.tile([P, C], F32, name="y")
+            total = stats.tile([P, 1], F32, name="total")
+            nc.vector.scalar_tensor_tensor(
+                out=y[:],
+                in0=z_of[n][:],
+                scalar=1.0,
+                in1=bias_all[:].rearrange("p t q -> p (t q)"),
+                op0=ALU.mult,
+                op1=ALU.add,
+                accum_out=total[:],
+            )
+            neg_mean = stats.tile([P, 1], F32, name="neg_mean")
+            nc.gpsimd.tensor_scalar(
+                out=neg_mean[:], in0=total[:], scalar1=-1.0 / C, scalar2=0.0, op0=ALU.mult, op1=ALU.add
+            )
+            unread = work.tile([P, C], BF16, name="unread")
+            squares = stats.tile([P, 1], F32, name="squares")
+            nc.scalar.activation(
+                out=unread[:], in_=y[:], func=ACT.Square, bias=neg_mean[:], scale=1.0, accum_out=squares[:]
+            )
+            rstd = stats.tile([P, 1], F32, name="rstd")
+            nc.scalar.activation(
+                out=rstd[:], in_=squares[:], func=ACT.Abs_reciprocal_sqrt, bias=EPS, scale=1.0 / C
+            )
+            y_of[n], neg_mean_of[n], rstd_of[n] = y, neg_mean, rstd
+
+        def normalise(n):
+            yn = work.tile([P, C], F32, name="yn", bufs=LAG + 3)
+            nc.gpsimd.tensor_scalar(
+                out=yn[:],
+                in0=y_of[n][:],
+                scalar1=neg_mean_of[n][:],
+                scalar2=rstd_of[n][:],
+                op0=ALU.add,
+                op1=ALU.mult,
+            )
+            normed_of[n] = yn
+
+        turned_of = {}
+
+        def turn(group):
+            for t in range(C_TILES):
+                turned = psum.tile([P, GROUP], F32, tag="turn")
+                for i in range(TILES):
+                    nc.tensor.transpose(
+                        turned[:, i * P : (i + 1) * P],
+                        normed_of[group * TILES + i][:, t * P : (t + 1) * P],
+                        ident[:],
+                    )
+                turned_of[(group, t)] = turned
+
+        def finish(group, t):
+            b, first = group * GROUP // N, group * GROUP % N
+            cols = slice(first, first + GROUP)
+            result = work.tile([P, GROUP], F32, name="result")
+            nc.vector.scalar_tensor_tensor(
+                out=result[:],
+                in0=turned_of[(group, t)][:],
+                scalar=gain[:, t : t + 1],
+                in1=xn_sb[b][:, t, cols],
+                op0=ALU.mult,
+                op1=ALU.add,
+            )
+            nc.sync.dma_start(out=out_rows[b, :, t, cols], in_=result[:])
+
+        for n in range(LEAD):
+            project(n)
+        for step in range(ALL_TILES + LAG):
+            if step + LEAD < ALL_TILES:
+                project(step + LEAD)
+            if step < ALL_TILES:
+                add_bias_and_measure(step)
+            if 1 <= step <= ALL_TILES:
+                normalise(step - 1)
+            if step >= LAG:
+                group, t = divmod(step - LAG, C_TILES)
+                if t == 0:
+                    turn(group)
+                finish(group, t)

@@ -19,10 +19,8 @@ PASSES = E // K_PASS
 C_TILES = C // P
 GROUP = 512
 TILES = GROUP // P
-HALVES = N // GROUP
 ALL_TILES = IMAGES * N // P
 EPS = 1e-5
-VECTOR_POSITIONS = 512
 LEAD = 3
 LAG = 7
 
@@ -66,10 +64,10 @@ def tile_linearattention_pb_kernel(tc, h_attn, xn, Wout, bout, outnorm_g, out):
             )
 
         w_raw = keep.tile([P, C_TILES, E], BF16)
-        load_h(0, 0)
-        nc.sync.dma_start(out=w_raw[:], in_=w_rows)
-        load_h(0, 1)
-        load_h(0, 2)
+        for g in range(PASSES):
+            k_cols = slice(g * K_PASS, (g + 1) * K_PASS)
+            load_h(0, g)
+            nc.sync.dma_start(out=w_raw[:, :, k_cols], in_=w_rows[:, :, k_cols])
         for g in range(PASSES):
             load_h(1, g)
         xn_sb = []
@@ -87,45 +85,40 @@ def tile_linearattention_pb_kernel(tc, h_attn, xn, Wout, bout, outnorm_g, out):
         warm_col = keep.tile([P, 1], F32)
         nc.scalar.activation(out=warm_col[:], in_=one_col[:], func=ACT.Abs_reciprocal_sqrt)
 
+        grouped_of = {}
         h_codes = {}
         h_scales = {}
 
         def regroup(b, g):
             raw = h_raw[(b, g)]
             grouped = stage.tile([P, N, PACK], BF16, align_bytes=64, name="grouped")
-            split = VECTOR_POSITIONS
             nc.vector.tensor_copy(
-                out=grouped[:, 0:split, :].rearrange("p (c i) t -> p c t i", i=4),
-                in_=raw[:, :, 0:split].rearrange("p t (c i) -> p c t i", i=4),
+                out=grouped[:, 0:GROUP, :].rearrange("p (c i) t -> p c t i", i=4),
+                in_=raw[:, :, 0:GROUP].rearrange("p t (c i) -> p c t i", i=4),
             )
             nc.scalar.copy(
-                out=grouped[:, split:N, :].rearrange("p (c i) t -> p c t i", i=4),
-                in_=raw[:, :, split:N].rearrange("p t (c i) -> p c t i", i=4),
+                out=grouped[:, GROUP:N, :].rearrange("p (c i) t -> p c t i", i=4),
+                in_=raw[:, :, GROUP:N].rearrange("p t (c i) -> p c t i", i=4),
             )
-            return grouped
+            grouped_of[(b, g)] = grouped
+            h_codes[(b, g)] = keep.tile([P, N], U32, align_bytes=64, name="h_codes_%d_%d" % (b, g))
+            h_scales[(b, g)] = keep.tile([P, N], U8, align_bytes=64, name="h_scales_%d_%d" % (b, g))
 
-        def quantise(b, g, grouped):
-            codes = keep.tile([P, N], U32, align_bytes=64, name="h_codes_%d_%d" % (b, g))
-            scales = keep.tile([P, N], U8, align_bytes=64, name="h_scales_%d_%d" % (b, g))
-            for half in range(HALVES):
-                cols = slice(half * GROUP, (half + 1) * GROUP)
-                nc.vector.quantize_mx(
-                    out=codes[:, cols].bitcast(FP8X4),
-                    scales=scales[:, cols],
-                    in_=grouped[:, cols, :].rearrange("p w j -> p (w j)"),
-                )
-            h_codes[(b, g)] = codes
-            h_scales[(b, g)] = scales
-
-        chunks = [(b, g) for b in range(IMAGES) for g in range(PASSES)]
-        quantise(0, 0, regroup(0, 0))
+        def quantise(b, g, half):
+            cols = slice(half * GROUP, (half + 1) * GROUP)
+            nc.vector.quantize_mx(
+                out=h_codes[(b, g)][:, cols].bitcast(FP8X4),
+                scales=h_scales[(b, g)][:, cols],
+                in_=grouped_of[(b, g)][:, cols, :].rearrange("p w j -> p (w j)"),
+            )
 
         w_words = w_raw[:].bitcast(F32).rearrange("p t (g q u) -> p t g u q", g=PASSES, u=2)
         w_grouped = keep.tile([P, PASSES, C, PACK], BF16, align_bytes=64)
         w_grouped_words = w_grouped[:].bitcast(F32)
         w_codes = keep.tile([P, PASSES, C], U32, align_bytes=64)
         w_scales = keep.tile([P, PASSES, C], U8, align_bytes=64)
-        for g in range(PASSES):
+
+        def turn_w(g):
             for pair in range(2):
                 turned = psum.tile([P, 2, 2, P], F32, tag="turn")
                 for tt in range(2):
@@ -137,25 +130,36 @@ def tile_linearattention_pb_kernel(tc, h_attn, xn, Wout, bout, outnorm_g, out):
                     ),
                     in_=turned[:].rearrange("p tt u c -> p tt c u"),
                 )
+
+        def quantise_w(g):
             nc.vector.quantize_mx(
                 out=w_codes[:, g, :].bitcast(FP8X4),
                 scales=w_scales[:, g, :],
                 in_=w_grouped[:, g, :, :].rearrange("p c j -> p (c j)"),
             )
 
-        bias_ps = psum.tile([P, C], F32, tag="turn")
-        nc.tensor.matmul(out=bias_ps[:], lhsT=ones[:], rhs=bias_row[:], start=True, stop=True)
         bias_all = keep.tile([P, C_TILES, P], F32)
-        nc.vector.tensor_copy(out=bias_all[:], in_=bias_ps[:].rearrange("p (q t) -> p t q", t=C_TILES))
         gain = keep.tile([P, C_TILES], F32)
-        nc.vector.tensor_copy(out=gain[:], in_=gain_bf[:])
 
-        waiting = regroup(*chunks[1])
-        for c in range(2, len(chunks)):
-            grouped = regroup(*chunks[c])
-            quantise(chunks[c - 1][0], chunks[c - 1][1], waiting)
-            waiting = grouped
-        quantise(chunks[-1][0], chunks[-1][1], waiting)
+        def spread_bias_and_gain():
+            bias_ps = psum.tile([P, C], F32, tag="turn")
+            nc.tensor.matmul(out=bias_ps[:], lhsT=ones[:], rhs=bias_row[:], start=True, stop=True)
+            nc.scalar.copy(out=bias_all[:], in_=bias_ps[:].rearrange("p (q t) -> p t q", t=C_TILES))
+            nc.gpsimd.tensor_copy(out=gain[:], in_=gain_bf[:])
+
+        earlier = None
+        for b, g in [(b, g) for b in range(IMAGES) for g in range(PASSES)]:
+            regroup(b, g)
+            if b == 0:
+                turn_w(g)
+            if earlier is not None:
+                quantise(earlier[0], earlier[1], 1)
+                if earlier[0] == 0:
+                    quantise_w(earlier[1])
+            quantise(b, g, 0)
+            earlier = (b, g)
+        quantise(earlier[0], earlier[1], 1)
+        spread_bias_and_gain()
 
         z_of = {}
         y_of = {}

@@ -19,9 +19,12 @@ PASSES = E // K_PASS
 C_TILES = C // P
 GROUP = 512
 TILES = GROUP // P
+HALVES = N // GROUP
 ALL_TILES = IMAGES * N // P
 EPS = 1e-5
+VECTOR_POSITIONS = 512
 LEAD = 3
+NORM_LAG = 2
 LAG = 7
 
 FLOPS = 2 * IMAGES * N * C * E
@@ -37,8 +40,8 @@ def tile_linearattention_pb_kernel(tc, h_attn, xn, Wout, bout, outnorm_g, out):
     with ExitStack() as ctx:
         keep = ctx.enter_context(tc.tile_pool(name="keep", bufs=1))
         stage = ctx.enter_context(tc.tile_pool(name="stage", bufs=3))
-        work = ctx.enter_context(tc.tile_pool(name="work", bufs=4))
-        stats = ctx.enter_context(tc.tile_pool(name="stats", bufs=4))
+        work = ctx.enter_context(tc.tile_pool(name="work", bufs=6))
+        stats = ctx.enter_context(tc.tile_pool(name="stats", bufs=6))
         psum = ctx.enter_context(tc.psum_pool(name="psum", bufs=4))
         ctx.enter_context(tc.manual_schedule())
 
@@ -64,10 +67,10 @@ def tile_linearattention_pb_kernel(tc, h_attn, xn, Wout, bout, outnorm_g, out):
             )
 
         w_raw = keep.tile([P, C_TILES, E], BF16)
-        for g in range(PASSES):
-            k_cols = slice(g * K_PASS, (g + 1) * K_PASS)
-            load_h(0, g)
-            nc.sync.dma_start(out=w_raw[:, :, k_cols], in_=w_rows[:, :, k_cols])
+        load_h(0, 0)
+        nc.sync.dma_start(out=w_raw[:], in_=w_rows)
+        load_h(0, 1)
+        load_h(0, 2)
         for g in range(PASSES):
             load_h(1, g)
         xn_sb = []
@@ -85,40 +88,45 @@ def tile_linearattention_pb_kernel(tc, h_attn, xn, Wout, bout, outnorm_g, out):
         warm_col = keep.tile([P, 1], F32)
         nc.scalar.activation(out=warm_col[:], in_=one_col[:], func=ACT.Abs_reciprocal_sqrt)
 
-        grouped_of = {}
         h_codes = {}
         h_scales = {}
 
         def regroup(b, g):
             raw = h_raw[(b, g)]
             grouped = stage.tile([P, N, PACK], BF16, align_bytes=64, name="grouped")
+            split = VECTOR_POSITIONS
             nc.vector.tensor_copy(
-                out=grouped[:, 0:GROUP, :].rearrange("p (c i) t -> p c t i", i=4),
-                in_=raw[:, :, 0:GROUP].rearrange("p t (c i) -> p c t i", i=4),
+                out=grouped[:, 0:split, :].rearrange("p (c i) t -> p c t i", i=4),
+                in_=raw[:, :, 0:split].rearrange("p t (c i) -> p c t i", i=4),
             )
             nc.scalar.copy(
-                out=grouped[:, GROUP:N, :].rearrange("p (c i) t -> p c t i", i=4),
-                in_=raw[:, :, GROUP:N].rearrange("p t (c i) -> p c t i", i=4),
+                out=grouped[:, split:N, :].rearrange("p (c i) t -> p c t i", i=4),
+                in_=raw[:, :, split:N].rearrange("p t (c i) -> p c t i", i=4),
             )
-            grouped_of[(b, g)] = grouped
-            h_codes[(b, g)] = keep.tile([P, N], U32, align_bytes=64, name="h_codes_%d_%d" % (b, g))
-            h_scales[(b, g)] = keep.tile([P, N], U8, align_bytes=64, name="h_scales_%d_%d" % (b, g))
+            return grouped
 
-        def quantise(b, g, half):
-            cols = slice(half * GROUP, (half + 1) * GROUP)
-            nc.vector.quantize_mx(
-                out=h_codes[(b, g)][:, cols].bitcast(FP8X4),
-                scales=h_scales[(b, g)][:, cols],
-                in_=grouped_of[(b, g)][:, cols, :].rearrange("p w j -> p (w j)"),
-            )
+        def quantise(b, g, grouped):
+            codes = keep.tile([P, N], U32, align_bytes=64, name="h_codes_%d_%d" % (b, g))
+            scales = keep.tile([P, N], U8, align_bytes=64, name="h_scales_%d_%d" % (b, g))
+            for half in range(HALVES):
+                cols = slice(half * GROUP, (half + 1) * GROUP)
+                nc.vector.quantize_mx(
+                    out=codes[:, cols].bitcast(FP8X4),
+                    scales=scales[:, cols],
+                    in_=grouped[:, cols, :].rearrange("p w j -> p (w j)"),
+                )
+            h_codes[(b, g)] = codes
+            h_scales[(b, g)] = scales
+
+        chunks = [(b, g) for b in range(IMAGES) for g in range(PASSES)]
+        quantise(0, 0, regroup(0, 0))
 
         w_words = w_raw[:].bitcast(F32).rearrange("p t (g q u) -> p t g u q", g=PASSES, u=2)
         w_grouped = keep.tile([P, PASSES, C, PACK], BF16, align_bytes=64)
         w_grouped_words = w_grouped[:].bitcast(F32)
         w_codes = keep.tile([P, PASSES, C], U32, align_bytes=64)
         w_scales = keep.tile([P, PASSES, C], U8, align_bytes=64)
-
-        def turn_w(g):
+        for g in range(PASSES):
             for pair in range(2):
                 turned = psum.tile([P, 2, 2, P], F32, tag="turn")
                 for tt in range(2):
@@ -130,40 +138,30 @@ def tile_linearattention_pb_kernel(tc, h_attn, xn, Wout, bout, outnorm_g, out):
                     ),
                     in_=turned[:].rearrange("p tt u c -> p tt c u"),
                 )
-
-        def quantise_w(g):
             nc.vector.quantize_mx(
                 out=w_codes[:, g, :].bitcast(FP8X4),
                 scales=w_scales[:, g, :],
                 in_=w_grouped[:, g, :, :].rearrange("p c j -> p (c j)"),
             )
 
+        bias_ps = psum.tile([P, C], F32, tag="turn")
+        nc.tensor.matmul(out=bias_ps[:], lhsT=ones[:], rhs=bias_row[:], start=True, stop=True)
         bias_all = keep.tile([P, C_TILES, P], F32)
+        nc.vector.tensor_copy(out=bias_all[:], in_=bias_ps[:].rearrange("p (q t) -> p t q", t=C_TILES))
         gain = keep.tile([P, C_TILES], F32)
+        nc.vector.tensor_copy(out=gain[:], in_=gain_bf[:])
 
-        def spread_bias_and_gain():
-            bias_ps = psum.tile([P, C], F32, tag="turn")
-            nc.tensor.matmul(out=bias_ps[:], lhsT=ones[:], rhs=bias_row[:], start=True, stop=True)
-            nc.scalar.copy(out=bias_all[:], in_=bias_ps[:].rearrange("p (q t) -> p t q", t=C_TILES))
-            nc.gpsimd.tensor_copy(out=gain[:], in_=gain_bf[:])
-
-        earlier = None
-        for b, g in [(b, g) for b in range(IMAGES) for g in range(PASSES)]:
-            regroup(b, g)
-            if b == 0:
-                turn_w(g)
-            if earlier is not None:
-                quantise(earlier[0], earlier[1], 1)
-                if earlier[0] == 0:
-                    quantise_w(earlier[1])
-            quantise(b, g, 0)
-            earlier = (b, g)
-        quantise(earlier[0], earlier[1], 1)
-        spread_bias_and_gain()
+        waiting = regroup(*chunks[1])
+        for c in range(2, len(chunks)):
+            grouped = regroup(*chunks[c])
+            quantise(chunks[c - 1][0], chunks[c - 1][1], waiting)
+            waiting = grouped
+        quantise(chunks[-1][0], chunks[-1][1], waiting)
 
         z_of = {}
         y_of = {}
         neg_mean_of = {}
+        squares_of = {}
         rstd_of = {}
         normed_of = {}
 
@@ -202,13 +200,16 @@ def tile_linearattention_pb_kernel(tc, h_attn, xn, Wout, bout, outnorm_g, out):
             unread = work.tile([P, C], BF16, name="unread")
             squares = stats.tile([P, 1], F32, name="squares")
             nc.scalar.activation(
-                out=unread[:], in_=y[:], func=ACT.Square, bias=neg_mean[:], scale=1.0, accum_out=squares[:]
+                out=unread[:], in_=y[:], func=ACT.Square, bias=total[:], scale=-1.0 * C, accum_out=squares[:]
             )
+            y_of[n], neg_mean_of[n], squares_of[n] = y, neg_mean, squares
+
+        def invert_deviation(n):
             rstd = stats.tile([P, 1], F32, name="rstd")
             nc.scalar.activation(
-                out=rstd[:], in_=squares[:], func=ACT.Abs_reciprocal_sqrt, bias=EPS, scale=1.0 / C
+                out=rstd[:], in_=squares_of[n][:], func=ACT.Abs_reciprocal_sqrt, bias=EPS, scale=1.0 / (C * C * C)
             )
-            y_of[n], neg_mean_of[n], rstd_of[n] = y, neg_mean, rstd
+            rstd_of[n] = rstd
 
         def normalise(n):
             yn = work.tile([P, C], F32, name="yn", bufs=LAG + 3)
@@ -256,8 +257,10 @@ def tile_linearattention_pb_kernel(tc, h_attn, xn, Wout, bout, outnorm_g, out):
                 project(step + LEAD)
             if step < ALL_TILES:
                 add_bias_and_measure(step)
-            if 1 <= step <= ALL_TILES:
-                normalise(step - 1)
+            if 0 <= step - 1 < ALL_TILES:
+                invert_deviation(step - 1)
+            if 0 <= step - NORM_LAG < ALL_TILES:
+                normalise(step - NORM_LAG)
             if step >= LAG:
                 group, t = divmod(step - LAG, C_TILES)
                 if t == 0:

@@ -20,12 +20,11 @@ C_TILES = C // P
 GROUP = 512
 TILES = GROUP // P
 HALVES = N // GROUP
-ALL_TILES = IMAGES * N // P
+GROUPS = IMAGES * HALVES
+ALL_TILES = GROUPS * TILES
+CHUNKS = IMAGES * PASSES
+BANKS = 8
 EPS = 1e-5
-VECTOR_POSITIONS = 512
-LEAD = 3
-NORM_LAG = 2
-LAG = 7
 
 FLOPS = 2 * IMAGES * N * C * E
 
@@ -39,10 +38,10 @@ def tile_linearattention_pb_kernel(tc, h_attn, xn, Wout, bout, outnorm_g, out):
 
     with ExitStack() as ctx:
         keep = ctx.enter_context(tc.tile_pool(name="keep", bufs=1))
-        stage = ctx.enter_context(tc.tile_pool(name="stage", bufs=3))
-        work = ctx.enter_context(tc.tile_pool(name="work", bufs=6))
-        stats = ctx.enter_context(tc.tile_pool(name="stats", bufs=6))
-        psum = ctx.enter_context(tc.psum_pool(name="psum", bufs=4))
+        stage = ctx.enter_context(tc.tile_pool(name="stage", bufs=2))
+        work = ctx.enter_context(tc.tile_pool(name="work", bufs=4))
+        stats = ctx.enter_context(tc.tile_pool(name="stats", bufs=ALL_TILES))
+        psum = ctx.enter_context(tc.psum_pool(name="psum", bufs=BANKS))
         ctx.enter_context(tc.manual_schedule())
 
         bias_row = keep.tile([P, C], BF16)
@@ -56,28 +55,43 @@ def tile_linearattention_pb_kernel(tc, h_attn, xn, Wout, bout, outnorm_g, out):
             )
 
         h_raw = {}
-        for b in range(IMAGES):
-            for g in range(PASSES):
-                h_raw[(b, g)] = keep.tile([P, PACK, N], BF16, name="h_raw_%d_%d" % (b, g))
+        w_raw = {}
+        xn_sb = {}
 
-        def load_h(b, g):
-            nc.sync.dma_start(
-                out=h_raw[(b, g)][:],
-                in_=h_rows[b, g * K_PASS : (g + 1) * K_PASS, :].rearrange("(p j) w -> p j w", j=PACK),
-            )
+        def h_source(c, cols):
+            b, g = divmod(c, PASSES)
+            return h_rows[b, g * K_PASS : (g + 1) * K_PASS, cols].rearrange("(p j) w -> p j w", j=PACK)
 
-        w_raw = keep.tile([P, C_TILES, E], BF16)
-        load_h(0, 0)
-        nc.sync.dma_start(out=w_raw[:], in_=w_rows)
-        load_h(0, 1)
-        load_h(0, 2)
-        for g in range(PASSES):
-            load_h(1, g)
-        xn_sb = []
+        def load_h_whole(c):
+            raw = keep.tile([P, PACK, N], BF16, name="h_raw_%d" % c)
+            nc.sync.dma_start(out=raw[:], in_=h_source(c, slice(0, N)))
+            for half in range(HALVES):
+                h_raw[(c, half)] = (raw, slice(half * GROUP, (half + 1) * GROUP))
+
+        def load_h_halves(c):
+            for half in range(HALVES):
+                raw = keep.tile([P, PACK, GROUP], BF16, name="h_raw_%d_%d" % (c, half))
+                nc.sync.dma_start(out=raw[:], in_=h_source(c, slice(half * GROUP, (half + 1) * GROUP)))
+                h_raw[(c, half)] = (raw, slice(0, GROUP))
+
+        def load_w(g):
+            raw = keep.tile([P, C_TILES, K_PASS], BF16, name="w_raw_%d" % g)
+            nc.sync.dma_start(out=raw[:], in_=w_rows[:, :, g * K_PASS : (g + 1) * K_PASS])
+            w_raw[g] = raw
+
+        load_h_halves(0)
+        load_w(0)
+        load_h_whole(1)
+        load_w(1)
+        load_h_whole(2)
+        load_w(2)
+        load_h_whole(3)
+        load_h_whole(4)
+        load_h_halves(5)
         for b in range(IMAGES):
             xn_b = keep.tile([P, C_TILES, N], BF16, name="xn_%d" % b)
             nc.sync.dma_start(out=xn_b[:], in_=xn_rows[b])
-            xn_sb.append(xn_b)
+            xn_sb[b] = xn_b
 
         ident = keep.tile([P, P], F32)
         make_identity(nc, ident[:])
@@ -90,73 +104,71 @@ def tile_linearattention_pb_kernel(tc, h_attn, xn, Wout, bout, outnorm_g, out):
 
         h_codes = {}
         h_scales = {}
+        grouped_of = {}
+        for c in range(CHUNKS):
+            h_codes[c] = keep.tile([P, N], U32, align_bytes=64, name="h_codes_%d" % c)
+            h_scales[c] = keep.tile([P, N], U8, align_bytes=64, name="h_scales_%d" % c)
 
-        def regroup(b, g):
-            raw = h_raw[(b, g)]
-            grouped = stage.tile([P, N, PACK], BF16, align_bytes=64, name="grouped")
-            split = VECTOR_POSITIONS
-            nc.vector.tensor_copy(
-                out=grouped[:, 0:split, :].rearrange("p (c i) t -> p c t i", i=4),
-                in_=raw[:, :, 0:split].rearrange("p t (c i) -> p c t i", i=4),
-            )
-            nc.scalar.copy(
-                out=grouped[:, split:N, :].rearrange("p (c i) t -> p c t i", i=4),
-                in_=raw[:, :, split:N].rearrange("p t (c i) -> p c t i", i=4),
-            )
-            return grouped
-
-        def quantise(b, g, grouped):
-            codes = keep.tile([P, N], U32, align_bytes=64, name="h_codes_%d_%d" % (b, g))
-            scales = keep.tile([P, N], U8, align_bytes=64, name="h_scales_%d_%d" % (b, g))
-            for half in range(HALVES):
-                cols = slice(half * GROUP, (half + 1) * GROUP)
-                nc.vector.quantize_mx(
-                    out=codes[:, cols].bitcast(FP8X4),
-                    scales=scales[:, cols],
-                    in_=grouped[:, cols, :].rearrange("p w j -> p (w j)"),
+        def regroup(c):
+            for half, engine_copy, name in ((0, nc.vector.tensor_copy, "by_vector"), (1, nc.scalar.copy, "by_scalar")):
+                raw, cols = h_raw[(c, half)]
+                grouped = stage.tile([P, GROUP, PACK], BF16, align_bytes=64, name=name)
+                engine_copy(
+                    out=grouped[:].rearrange("p (c i) t -> p c t i", i=4),
+                    in_=raw[:, :, cols].rearrange("p t (c i) -> p c t i", i=4),
                 )
-            h_codes[(b, g)] = codes
-            h_scales[(b, g)] = scales
+                grouped_of[(c, half)] = grouped
 
-        chunks = [(b, g) for b in range(IMAGES) for g in range(PASSES)]
-        quantise(0, 0, regroup(0, 0))
+        def quantise(c, half):
+            cols = slice(half * GROUP, (half + 1) * GROUP)
+            nc.vector.quantize_mx(
+                out=h_codes[c][:, cols].bitcast(FP8X4),
+                scales=h_scales[c][:, cols],
+                in_=grouped_of[(c, half)][:].rearrange("p w j -> p (w j)"),
+            )
 
-        w_words = w_raw[:].bitcast(F32).rearrange("p t (g q u) -> p t g u q", g=PASSES, u=2)
         w_grouped = keep.tile([P, PASSES, C, PACK], BF16, align_bytes=64)
         w_grouped_words = w_grouped[:].bitcast(F32)
         w_codes = keep.tile([P, PASSES, C], U32, align_bytes=64)
         w_scales = keep.tile([P, PASSES, C], U8, align_bytes=64)
-        for g in range(PASSES):
+
+        def w_turn(g):
+            w_words = w_raw[g][:].bitcast(F32).rearrange("p t (q u) -> p t u q", u=2)
             for pair in range(2):
-                turned = psum.tile([P, 2, 2, P], F32, tag="turn")
+                turned = psum.tile([P, 2, 2, P], F32, tag="bank")
                 for tt in range(2):
                     for u in range(2):
-                        nc.tensor.transpose(turned[:, tt, u, :], w_words[:, 2 * pair + tt, g, u, :], ident[:])
+                        nc.tensor.transpose(turned[:, tt, u, :], w_words[:, 2 * pair + tt, u, :], ident[:])
                 nc.scalar.copy(
                     out=w_grouped_words[:, g, 2 * pair * P : (2 * pair + 2) * P, :].rearrange(
                         "p (tt c) u -> p tt c u", tt=2
                     ),
                     in_=turned[:].rearrange("p tt u c -> p tt c u"),
                 )
+
+        def w_quantise(g):
             nc.vector.quantize_mx(
                 out=w_codes[:, g, :].bitcast(FP8X4),
                 scales=w_scales[:, g, :],
                 in_=w_grouped[:, g, :, :].rearrange("p c j -> p (c j)"),
             )
 
-        bias_ps = psum.tile([P, C], F32, tag="turn")
-        nc.tensor.matmul(out=bias_ps[:], lhsT=ones[:], rhs=bias_row[:], start=True, stop=True)
         bias_all = keep.tile([P, C_TILES, P], F32)
-        nc.vector.tensor_copy(out=bias_all[:], in_=bias_ps[:].rearrange("p (q t) -> p t q", t=C_TILES))
         gain = keep.tile([P, C_TILES], F32)
-        nc.vector.tensor_copy(out=gain[:], in_=gain_bf[:])
-
-        waiting = regroup(*chunks[1])
-        for c in range(2, len(chunks)):
-            grouped = regroup(*chunks[c])
-            quantise(chunks[c - 1][0], chunks[c - 1][1], waiting)
-            waiting = grouped
-        quantise(chunks[-1][0], chunks[-1][1], waiting)
+        for c in range(CHUNKS):
+            regroup(c)
+            if c > 0:
+                quantise(c - 1, 1)
+            quantise(c, 0)
+            if 1 <= c <= PASSES:
+                w_quantise(c - 1)
+            if c < PASSES:
+                w_turn(c)
+            if c == PASSES:
+                bias_ps = psum.tile([P, C], F32, tag="bank")
+                nc.tensor.matmul(out=bias_ps[:], lhsT=ones[:], rhs=bias_row[:], start=True, stop=True)
+                nc.vector.tensor_copy(out=bias_all[:], in_=bias_ps[:].rearrange("p (q t) -> p t q", t=C_TILES))
+                nc.vector.tensor_copy(out=gain[:], in_=gain_bf[:])
 
         z_of = {}
         y_of = {}
@@ -168,12 +180,13 @@ def tile_linearattention_pb_kernel(tc, h_attn, xn, Wout, bout, outnorm_g, out):
         def project(n):
             b, first = n * P // N, n * P % N
             cols = slice(first, first + P)
-            z = psum.tile([P, C], F32, tag="z")
+            z = psum.tile([P, C], F32, tag="bank")
             for g in range(PASSES):
+                c = b * PASSES + g
                 nc.tensor.matmul_mx(
                     out=z[:],
-                    lhsT=h_codes[(b, g)][:, cols].bitcast(FP8X4),
-                    lhsT_scale=h_scales[(b, g)][:, cols],
+                    lhsT=h_codes[c][:, cols].bitcast(FP8X4),
+                    lhsT_scale=h_scales[c][:, cols],
                     rhs=w_codes[:, g, :].bitcast(FP8X4),
                     rhs_scale=w_scales[:, g, :],
                     start=(g == 0),
@@ -182,7 +195,7 @@ def tile_linearattention_pb_kernel(tc, h_attn, xn, Wout, bout, outnorm_g, out):
             z_of[n] = z
 
         def add_bias_and_measure(n):
-            y = work.tile([P, C], F32, name="y")
+            y = work.tile([P, C], F32, name="y", bufs=6)
             total = stats.tile([P, 1], F32, name="total")
             nc.vector.scalar_tensor_tensor(
                 out=y[:],
@@ -197,7 +210,7 @@ def tile_linearattention_pb_kernel(tc, h_attn, xn, Wout, bout, outnorm_g, out):
             nc.gpsimd.tensor_scalar(
                 out=neg_mean[:], in0=total[:], scalar1=-1.0 / C, scalar2=0.0, op0=ALU.mult, op1=ALU.add
             )
-            unread = work.tile([P, C], BF16, name="unread")
+            unread = work.tile([P, C], BF16, name="unread", bufs=2)
             squares = stats.tile([P, 1], F32, name="squares")
             nc.scalar.activation(
                 out=unread[:], in_=y[:], func=ACT.Square, bias=total[:], scale=-1.0 * C, accum_out=squares[:]
@@ -212,22 +225,37 @@ def tile_linearattention_pb_kernel(tc, h_attn, xn, Wout, bout, outnorm_g, out):
             rstd_of[n] = rstd
 
         def normalise(n):
-            yn = work.tile([P, C], F32, name="yn", bufs=LAG + 3)
-            nc.gpsimd.tensor_scalar(
-                out=yn[:],
-                in0=y_of[n][:],
-                scalar1=neg_mean_of[n][:],
-                scalar2=rstd_of[n][:],
-                op0=ALU.add,
-                op1=ALU.mult,
-            )
+            yn = work.tile([P, C], F32, name="yn", bufs=12)
+            if n % 2 == 0:
+                nc.gpsimd.tensor_scalar(
+                    out=yn[:],
+                    in0=y_of[n][:],
+                    scalar1=neg_mean_of[n][:],
+                    scalar2=rstd_of[n][:],
+                    op0=ALU.add,
+                    op1=ALU.mult,
+                )
+            else:
+                shift = stats.tile([P, 1], F32, name="shift")
+                nc.gpsimd.tensor_scalar(
+                    out=shift[:], in0=neg_mean_of[n][:], scalar1=rstd_of[n][:], scalar2=0.0, op0=ALU.mult, op1=ALU.add
+                )
+                nc.scalar.activation(out=yn[:], in_=y_of[n][:], func=ACT.Identity, bias=shift[:], scale=rstd_of[n][:])
             normed_of[n] = yn
+
+        def measure(n):
+            if n < ALL_TILES:
+                add_bias_and_measure(n)
+            if 0 <= n - 1 < ALL_TILES:
+                invert_deviation(n - 1)
+            if 0 <= n - 2 < ALL_TILES:
+                normalise(n - 2)
 
         turned_of = {}
 
         def turn(group):
             for t in range(C_TILES):
-                turned = psum.tile([P, GROUP], F32, tag="turn")
+                turned = psum.tile([P, GROUP], F32, tag="bank")
                 for i in range(TILES):
                     nc.tensor.transpose(
                         turned[:, i * P : (i + 1) * P],
@@ -236,33 +264,36 @@ def tile_linearattention_pb_kernel(tc, h_attn, xn, Wout, bout, outnorm_g, out):
                     )
                 turned_of[(group, t)] = turned
 
-        def finish(group, t):
+        def finish(group):
             b, first = group * GROUP // N, group * GROUP % N
             cols = slice(first, first + GROUP)
-            result = work.tile([P, GROUP], F32, name="result")
-            nc.vector.scalar_tensor_tensor(
-                out=result[:],
-                in0=turned_of[(group, t)][:],
-                scalar=gain[:, t : t + 1],
-                in1=xn_sb[b][:, t, cols],
-                op0=ALU.mult,
-                op1=ALU.add,
-            )
-            nc.sync.dma_start(out=out_rows[b, :, t, cols], in_=result[:])
+            for t in range(C_TILES):
+                result = work.tile([P, GROUP], F32, name="result")
+                nc.vector.scalar_tensor_tensor(
+                    out=result[:],
+                    in0=turned_of[(group, t)][:],
+                    scalar=gain[:, t : t + 1],
+                    in1=xn_sb[b][:, t, cols],
+                    op0=ALU.mult,
+                    op1=ALU.add,
+                )
+                nc.sync.dma_start(out=out_rows[b, :, t, cols], in_=result[:])
 
-        for n in range(LEAD):
+        for n in range(2 * TILES):
             project(n)
-        for step in range(ALL_TILES + LAG):
-            if step + LEAD < ALL_TILES:
-                project(step + LEAD)
-            if step < ALL_TILES:
-                add_bias_and_measure(step)
-            if 0 <= step - 1 < ALL_TILES:
-                invert_deviation(step - 1)
-            if 0 <= step - NORM_LAG < ALL_TILES:
-                normalise(step - NORM_LAG)
-            if step >= LAG:
-                group, t = divmod(step - LAG, C_TILES)
-                if t == 0:
-                    turn(group)
-                finish(group, t)
+        for n in range(TILES):
+            measure(n)
+        quantise(CHUNKS - 1, 1)
+        for n in range(2 * TILES, 3 * TILES):
+            project(n)
+        for n in range(TILES, 3 * TILES):
+            measure(n)
+        turn(0)
+        for n in range(3 * TILES, ALL_TILES):
+            project(n)
+        finish(0)
+        for n in range(3 * TILES, ALL_TILES + 2):
+            measure(n)
+        for group in range(1, GROUPS):
+            turn(group)
+            finish(group)

@@ -25,6 +25,8 @@ ALL_TILES = GROUPS * TILES
 CHUNKS = IMAGES * PASSES
 BANKS = 8
 EPS = 1e-5
+HELPED = 3
+HELPED_GROUPS = (1, 2)
 
 FLOPS = 2 * IMAGES * N * C * E
 
@@ -80,12 +82,12 @@ def tile_linearattention_pb_kernel(tc, h_attn, xn, Wout, bout, outnorm_g, out):
             w_raw[g] = raw
 
         load_h_halves(0)
-        load_w(0)
         load_h_whole(1)
-        load_w(1)
+        load_w(0)
         load_h_whole(2)
-        load_w(2)
+        load_w(1)
         load_h_whole(3)
+        load_w(2)
         load_h_whole(4)
         load_h_halves(5)
         for b in range(IMAGES):
@@ -160,11 +162,11 @@ def tile_linearattention_pb_kernel(tc, h_attn, xn, Wout, bout, outnorm_g, out):
             if c > 0:
                 quantise(c - 1, 1)
             quantise(c, 0)
+            if 2 <= c <= PASSES + 1:
+                w_quantise(c - 2)
             if 1 <= c <= PASSES:
-                w_quantise(c - 1)
-            if c < PASSES:
-                w_turn(c)
-            if c == PASSES:
+                w_turn(c - 1)
+            if c == PASSES + 1:
                 bias_ps = psum.tile([P, C], F32, tag="bank")
                 nc.tensor.matmul(out=bias_ps[:], lhsT=ones[:], rhs=bias_row[:], start=True, stop=True)
                 nc.vector.tensor_copy(out=bias_all[:], in_=bias_ps[:].rearrange("p (q t) -> p t q", t=C_TILES))
@@ -264,10 +266,20 @@ def tile_linearattention_pb_kernel(tc, h_attn, xn, Wout, bout, outnorm_g, out):
                     )
                 turned_of[(group, t)] = turned
 
-        def finish(group):
+        helped_of = {}
+
+        def place(group):
             b, first = group * GROUP // N, group * GROUP % N
-            cols = slice(first, first + GROUP)
-            for t in range(C_TILES):
+            return b, slice(first, first + GROUP)
+
+        def store_helped(group):
+            b, cols = place(group)
+            nc.scalar.dma_start(out=out_rows[b, :, HELPED, cols], in_=helped_of[group][:])
+
+        def finish(group):
+            b, cols = place(group)
+            helped_here = group in HELPED_GROUPS
+            for t in [t for t in range(C_TILES) if not (helped_here and t == HELPED)]:
                 result = work.tile([P, GROUP], F32, name="result")
                 nc.vector.scalar_tensor_tensor(
                     out=result[:],
@@ -278,6 +290,16 @@ def tile_linearattention_pb_kernel(tc, h_attn, xn, Wout, bout, outnorm_g, out):
                     op1=ALU.add,
                 )
                 nc.sync.dma_start(out=out_rows[b, :, t, cols], in_=result[:])
+            if helped_here:
+                scaled = work.tile([P, GROUP], F32, name="scaled", bufs=2)
+                nc.scalar.activation(
+                    out=scaled[:], in_=turned_of[(group, HELPED)][:], func=ACT.Copy, scale=gain[:, HELPED : HELPED + 1]
+                )
+                helped = work.tile([P, GROUP], F32, name="helped", bufs=2)
+                nc.gpsimd.tensor_tensor(out=helped[:], in0=scaled[:], in1=xn_sb[b][:, HELPED, cols], op=ALU.add)
+                helped_of[group] = helped
+            if group - 1 in HELPED_GROUPS:
+                store_helped(group - 1)
 
         for n in range(2 * TILES):
             project(n)

@@ -40,7 +40,7 @@ def tile_linearattention_pb_kernel(tc, h_attn, xn, Wout, bout, outnorm_g, out):
 
     with ExitStack() as ctx:
         keep = ctx.enter_context(tc.tile_pool(name="keep", bufs=1))
-        stage = ctx.enter_context(tc.tile_pool(name="stage", bufs=2))
+        stage = ctx.enter_context(tc.tile_pool(name="stage", bufs=3))
         work = ctx.enter_context(tc.tile_pool(name="work", bufs=4))
         stats = ctx.enter_context(tc.tile_pool(name="stats", bufs=ALL_TILES))
         psum = ctx.enter_context(tc.psum_pool(name="psum", bufs=BANKS))
@@ -197,7 +197,7 @@ def tile_linearattention_pb_kernel(tc, h_attn, xn, Wout, bout, outnorm_g, out):
             z_of[n] = z
 
         def add_bias_and_measure(n):
-            y = work.tile([P, C], F32, name="y", bufs=6)
+            y = work.tile([P, C], F32, name="y", bufs=8)
             total = stats.tile([P, 1], F32, name="total")
             nc.vector.scalar_tensor_tensor(
                 out=y[:],
@@ -227,7 +227,7 @@ def tile_linearattention_pb_kernel(tc, h_attn, xn, Wout, bout, outnorm_g, out):
             rstd_of[n] = rstd
 
         def normalise(n):
-            yn = work.tile([P, C], F32, name="yn", bufs=12)
+            yn = work.tile([P, C], F32, name="yn", bufs=ALL_TILES)
             if n % 2 == 0:
                 nc.gpsimd.tensor_scalar(
                     out=yn[:],
@@ -280,7 +280,7 @@ def tile_linearattention_pb_kernel(tc, h_attn, xn, Wout, bout, outnorm_g, out):
             b, cols = place(group)
             helped_here = group in HELPED_GROUPS
             for t in [t for t in range(C_TILES) if not (helped_here and t == HELPED)]:
-                result = work.tile([P, GROUP], F32, name="result")
+                result = work.tile([P, GROUP], F32, name="result", bufs=10)
                 nc.vector.scalar_tensor_tensor(
                     out=result[:],
                     in0=turned_of[(group, t)][:],

@@ -70,18 +70,12 @@ def tile_linearattention_pb_kernel(tc, h_attn, xn, Wout, bout, outnorm_g, out):
             for half in range(HALVES):
                 h_raw[(c, half)] = (raw, slice(half * GROUP, (half + 1) * GROUP))
 
-        def load_h_halves(c):
-            for half in range(HALVES):
-                raw = keep.tile([P, PACK, GROUP], BF16, name="h_raw_%d_%d" % (c, half))
-                nc.sync.dma_start(out=raw[:], in_=h_source(c, slice(half * GROUP, (half + 1) * GROUP)))
-                h_raw[(c, half)] = (raw, slice(0, GROUP))
-
         def load_w(g):
             raw = keep.tile([P, C_TILES, K_PASS], BF16, name="w_raw_%d" % g)
             nc.sync.dma_start(out=raw[:], in_=w_rows[:, :, g * K_PASS : (g + 1) * K_PASS])
             w_raw[g] = raw
 
-        load_h_halves(0)
+        load_h_whole(0)
         load_h_whole(1)
         load_w(0)
         load_h_whole(2)
@@ -89,7 +83,7 @@ def tile_linearattention_pb_kernel(tc, h_attn, xn, Wout, bout, outnorm_g, out):
         load_h_whole(3)
         load_w(2)
         load_h_whole(4)
-        load_h_halves(5)
+        load_h_whole(5)
         for b in range(IMAGES):
             xn_b = keep.tile([P, C_TILES, N], BF16, name="xn_%d" % b)
             nc.sync.dma_start(out=xn_b[:], in_=xn_rows[b])

@@ -44,7 +44,6 @@ def tile_linearattention_pb_kernel(tc, h_attn, xn, Wout, bout, outnorm_g, out):
         work = ctx.enter_context(tc.tile_pool(name="work", bufs=4))
         stats = ctx.enter_context(tc.tile_pool(name="stats", bufs=ALL_TILES))
         psum = ctx.enter_context(tc.psum_pool(name="psum", bufs=BANKS))
-        ctx.enter_context(tc.manual_schedule())
 
         bias_row = keep.tile([P, C], BF16)
         nc.vector.memset(bias_row[:], 0.0)

@@ -26,7 +26,7 @@ CHUNKS = IMAGES * PASSES
 BANKS = 8
 EPS = 1e-5
 HELPED = 3
-HELPED_GROUPS = (1, 2)
+HELPED_GROUPS = ()
 
 FLOPS = 2 * IMAGES * N * C * E
 
@@ -150,20 +150,12 @@ def tile_linearattention_pb_kernel(tc, h_attn, xn, Wout, bout, outnorm_g, out):
 
         bias_all = keep.tile([P, C_TILES, P], F32)
         gain = keep.tile([P, C_TILES], F32)
-        for c in range(CHUNKS):
-            regroup(c)
-            if c > 0:
-                quantise(c - 1, 1)
-            quantise(c, 0)
-            if 2 <= c <= PASSES + 1:
-                w_quantise(c - 2)
-            if 1 <= c <= PASSES:
-                w_turn(c - 1)
-            if c == PASSES + 1:
-                bias_ps = psum.tile([P, C], F32, tag="bank")
-                nc.tensor.matmul(out=bias_ps[:], lhsT=ones[:], rhs=bias_row[:], start=True, stop=True)
-                nc.vector.tensor_copy(out=bias_all[:], in_=bias_ps[:].rearrange("p (q t) -> p t q", t=C_TILES))
-                nc.vector.tensor_copy(out=gain[:], in_=gain_bf[:])
+
+        def spread_bias():
+            bias_ps = psum.tile([P, C], F32, tag="bank")
+            nc.tensor.matmul(out=bias_ps[:], lhsT=ones[:], rhs=bias_row[:], start=True, stop=True)
+            nc.vector.tensor_copy(out=bias_all[:], in_=bias_ps[:].rearrange("p (q t) -> p t q", t=C_TILES))
+            nc.vector.tensor_copy(out=gain[:], in_=gain_bf[:])
 
         z_of = {}
         y_of = {}
@@ -294,6 +286,17 @@ def tile_linearattention_pb_kernel(tc, h_attn, xn, Wout, bout, outnorm_g, out):
             if group - 1 in HELPED_GROUPS:
                 store_helped(group - 1)
 
+        for c in range(CHUNKS):
+            regroup(c)
+            if c > 0:
+                quantise(c - 1, 1)
+            quantise(c, 0)
+            if 2 <= c <= PASSES + 1:
+                w_quantise(c - 2)
+            if 1 <= c < PASSES + 1:
+                w_turn(c - 1)
+            if c == PASSES + 1:
+                spread_bias()
         for n in range(2 * TILES):
             project(n)
         for n in range(TILES):

@@ -194,9 +194,7 @@ def tile_linearattention_pb_kernel(tc, h_attn, xn, Wout, bout, outnorm_g, out):
                 accum_out=total[:],
             )
             neg_mean = stats.tile([P, 1], F32, name="neg_mean")
-            nc.gpsimd.tensor_scalar(
-                out=neg_mean[:], in0=total[:], scalar1=-1.0 / C, scalar2=0.0, op0=ALU.mult, op1=ALU.add
-            )
+            nc.scalar.activation(out=neg_mean[:], in_=total[:], func=ACT.Copy, scale=-1.0 / C)
             unread = work.tile([P, C], BF16, name="unread", bufs=2)
             squares = stats.tile([P, 1], F32, name="squares")
             nc.scalar.activation(
@@ -213,7 +211,7 @@ def tile_linearattention_pb_kernel(tc, h_attn, xn, Wout, bout, outnorm_g, out):
 
         def normalise(n):
             yn = work.tile([P, C], F32, name="yn", bufs=ALL_TILES)
-            if n % 2 == 0:
+            if n % 2 == 0 or True:
                 nc.gpsimd.tensor_scalar(
                     out=yn[:],
                     in0=y_of[n][:],

@@ -25,6 +25,9 @@ ALL_TILES = GROUPS * TILES
 CHUNKS = IMAGES * PASSES
 BANKS = 8
 EPS = 1e-5
+EARLY_SHARE = 576
+LATE_SHARE = 384
+LATE_CHUNKS = 2
 HELPED = 3
 HELPED_GROUPS = ()
 
@@ -105,21 +108,28 @@ def tile_linearattention_pb_kernel(tc, h_attn, xn, Wout, bout, outnorm_g, out):
             h_scales[c] = keep.tile([P, N], U8, align_bytes=64, name="h_scales_%d" % c)
 
         def regroup(c):
-            for half, engine_copy, name in ((0, nc.vector.tensor_copy, "by_vector"), (1, nc.scalar.copy, "by_scalar")):
-                raw, cols = h_raw[(c, half)]
-                grouped = stage.tile([P, GROUP, PACK], BF16, align_bytes=64, name=name)
+            raw = h_raw[(c, 0)][0]
+            share = EARLY_SHARE if c < CHUNKS - LATE_CHUNKS else LATE_SHARE
+            grouped = stage.tile([P, N, PACK], BF16, align_bytes=64, name="grouped")
+            pieces = [(nc.vector.tensor_copy, 0, min(share, GROUP))]
+            if share < GROUP:
+                pieces.append((nc.scalar.copy, share, GROUP))
+            pieces.append((nc.scalar.copy, max(share, GROUP), N))
+            if share > GROUP:
+                pieces.append((nc.vector.tensor_copy, GROUP, share))
+            for engine_copy, first, last in pieces:
                 engine_copy(
-                    out=grouped[:].rearrange("p (c i) t -> p c t i", i=4),
-                    in_=raw[:, :, cols].rearrange("p t (c i) -> p c t i", i=4),
+                    out=grouped[:, first:last, :].rearrange("p (c i) t -> p c t i", i=4),
+                    in_=raw[:, :, first:last].rearrange("p t (c i) -> p c t i", i=4),
                 )
-                grouped_of[(c, half)] = grouped
+            grouped_of[c] = grouped
 
         def quantise(c, half):
             cols = slice(half * GROUP, (half + 1) * GROUP)
             nc.vector.quantize_mx(
                 out=h_codes[c][:, cols].bitcast(FP8X4),
                 scales=h_scales[c][:, cols],
-                in_=grouped_of[(c, half)][:].rearrange("p w j -> p (w j)"),
+                in_=grouped_of[c][:, cols, :].rearrange("p w j -> p (w j)"),
             )
 
         w_grouped = keep.tile([P, PASSES, C, PACK], BF16, align_bytes=64)

from contextlib import ExitStack

import concourse.mybir as mybir
from concourse.masks import make_identity

F32 = mybir.dt.float32
BF16 = mybir.dt.bfloat16
U32 = mybir.dt.uint32
U8 = mybir.dt.uint8
FP8X4 = mybir.dt.float8_e4m3fn_x4
ALU = mybir.AluOpType
ACT = mybir.ActivationFunctionType

P = 128
PACK = 4
K_PASS = P * PACK
IMAGES, C, E, N = 2, 512, 1536, 1024
PASSES = E // K_PASS
C_TILES = C // P
GROUP = 512
TILES = GROUP // P
HALVES = N // GROUP
GROUPS = IMAGES * HALVES
ALL_TILES = GROUPS * TILES
CHUNKS = IMAGES * PASSES
BANKS = 8
EPS = 1e-5
EARLY_SHARE = 576
LATE_SHARE = 384
LATE_CHUNKS = 2
HELPED = 3
HELPED_GROUPS = ()

FLOPS = 2 * IMAGES * N * C * E


def tile_linearattention_pb_kernel(tc, h_attn, xn, Wout, bout, outnorm_g, out):
    nc = tc.nc
    h_rows = h_attn.rearrange("b e y x -> b e (y x)")
    xn_rows = xn.rearrange("b (p t) y x -> b p t (y x)", t=C_TILES)
    out_rows = out.rearrange("b (p t) y x -> b p t (y x)", t=C_TILES)
    w_rows = Wout.rearrange("(p t) e -> p t e", t=C_TILES)

    with ExitStack() as ctx:
        keep = ctx.enter_context(tc.tile_pool(name="keep", bufs=1))
        stage = ctx.enter_context(tc.tile_pool(name="stage", bufs=3))
        work = ctx.enter_context(tc.tile_pool(name="work", bufs=4))
        stats = ctx.enter_context(tc.tile_pool(name="stats", bufs=ALL_TILES))
        psum = ctx.enter_context(tc.psum_pool(name="psum", bufs=BANKS))

        bias_row = keep.tile([P, C], BF16)
        nc.vector.memset(bias_row[:], 0.0)
        nc.scalar.dma_start(out=bias_row[0:1, :], in_=bout.rearrange("(o c) -> o c", o=1))
        gain_bf = keep.tile([P, C_TILES], BF16)
        with nc.allow_non_contiguous_dma(reason="four gains to a partition"):
            nc.scalar.dma_start(
                out=gain_bf[:],
                in_=outnorm_g.rearrange("o c y x -> (o c y x)").rearrange("(p t) -> p t", t=C_TILES),
            )

        h_raw = {}
        w_raw = {}
        xn_sb = {}

        def h_source(c, cols):
            b, g = divmod(c, PASSES)
            return h_rows[b, g * K_PASS : (g + 1) * K_PASS, cols].rearrange("(p j) w -> p j w", j=PACK)

        def load_h_whole(c):
            raw = keep.tile([P, PACK, N], BF16, name="h_raw_%d" % c)
            nc.sync.dma_start(out=raw[:], in_=h_source(c, slice(0, N)))
            for half in range(HALVES):
                h_raw[(c, half)] = (raw, slice(half * GROUP, (half + 1) * GROUP))

        def load_w(g):
            raw = keep.tile([P, C_TILES, K_PASS], BF16, name="w_raw_%d" % g)
            nc.sync.dma_start(out=raw[:], in_=w_rows[:, :, g * K_PASS : (g + 1) * K_PASS])
            w_raw[g] = raw

        load_h_whole(0)
        load_h_whole(1)
        load_w(0)
        load_h_whole(2)
        load_w(1)
        load_h_whole(3)
        load_w(2)
        load_h_whole(4)
        load_h_whole(5)
        for b in range(IMAGES):
            xn_b = keep.tile([P, C_TILES, N], BF16, name="xn_%d" % b)
            nc.sync.dma_start(out=xn_b[:], in_=xn_rows[b])
            xn_sb[b] = xn_b

        ident = keep.tile([P, P], F32)
        make_identity(nc, ident[:])
        ones = keep.tile([P, P], BF16)
        nc.vector.memset(ones[:], 1.0)
        one_col = keep.tile([P, 1], F32)
        nc.vector.memset(one_col[:], 1.0)
        warm_col = keep.tile([P, 1], F32)
        nc.scalar.activation(out=warm_col[:], in_=one_col[:], func=ACT.Abs_reciprocal_sqrt)

        h_codes = {}
        h_scales = {}
        grouped_of = {}
        for c in range(CHUNKS):
            h_codes[c] = keep.tile([P, N], U32, align_bytes=64, name="h_codes_%d" % c)
            h_scales[c] = keep.tile([P, N], U8, align_bytes=64, name="h_scales_%d" % c)

        def regroup(c):
            raw = h_raw[(c, 0)][0]
            share = EARLY_SHARE if c < CHUNKS - LATE_CHUNKS else LATE_SHARE
            grouped = stage.tile([P, N, PACK], BF16, align_bytes=64, name="grouped")
            pieces = [(nc.vector.tensor_copy, 0, min(share, GROUP))]
            if share < GROUP:
                pieces.append((nc.scalar.copy, share, GROUP))
            pieces.append((nc.scalar.copy, max(share, GROUP), N))
            if share > GROUP:
                pieces.append((nc.vector.tensor_copy, GROUP, share))
            for engine_copy, first, last in pieces:
                engine_copy(
                    out=grouped[:, first:last, :].rearrange("p (c i) t -> p c t i", i=4),
                    in_=raw[:, :, first:last].rearrange("p t (c i) -> p c t i", i=4),
                )
            grouped_of[c] = grouped

        def quantise(c, half):
            cols = slice(half * GROUP, (half + 1) * GROUP)
            nc.vector.quantize_mx(
                out=h_codes[c][:, cols].bitcast(FP8X4),
                scales=h_scales[c][:, cols],
                in_=grouped_of[c][:, cols, :].rearrange("p w j -> p (w j)"),
            )

        w_grouped = keep.tile([P, PASSES, C, PACK], BF16, align_bytes=64)
        w_grouped_words = w_grouped[:].bitcast(F32)
        w_codes = keep.tile([P, PASSES, C], U32, align_bytes=64)
        w_scales = keep.tile([P, PASSES, C], U8, align_bytes=64)

        def w_turn(g):
            w_words = w_raw[g][:].bitcast(F32).rearrange("p t (q u) -> p t u q", u=2)
            for pair in range(2):
                turned = psum.tile([P, 2, 2, P], F32, tag="bank")
                for tt in range(2):
                    for u in range(2):
                        nc.tensor.transpose(turned[:, tt, u, :], w_words[:, 2 * pair + tt, u, :], ident[:])
                nc.scalar.copy(
                    out=w_grouped_words[:, g, 2 * pair * P : (2 * pair + 2) * P, :].rearrange(
                        "p (tt c) u -> p tt c u", tt=2
                    ),
                    in_=turned[:].rearrange("p tt u c -> p tt c u"),
                )

        def w_quantise(g):
            nc.vector.quantize_mx(
                out=w_codes[:, g, :].bitcast(FP8X4),
                scales=w_scales[:, g, :],
                in_=w_grouped[:, g, :, :].rearrange("p c j -> p (c j)"),
            )

        bias_all = keep.tile([P, C_TILES, P], F32)
        gain = keep.tile([P, C_TILES], F32)

        def spread_bias():
            bias_ps = psum.tile([P, C], F32, tag="bank")
            nc.tensor.matmul(out=bias_ps[:], lhsT=ones[:], rhs=bias_row[:], start=True, stop=True)
            nc.vector.tensor_copy(out=bias_all[:], in_=bias_ps[:].rearrange("p (q t) -> p t q", t=C_TILES))
            nc.vector.tensor_copy(out=gain[:], in_=gain_bf[:])

        z_of = {}
        y_of = {}
        neg_mean_of = {}
        squares_of = {}
        rstd_of = {}
        normed_of = {}

        def project(n):
            b, first = n * P // N, n * P % N
            cols = slice(first, first + P)
            z = psum.tile([P, C], F32, tag="bank")
            for g in range(PASSES):
                c = b * PASSES + g
                nc.tensor.matmul_mx(
                    out=z[:],
                    lhsT=h_codes[c][:, cols].bitcast(FP8X4),
                    lhsT_scale=h_scales[c][:, cols],
                    rhs=w_codes[:, g, :].bitcast(FP8X4),
                    rhs_scale=w_scales[:, g, :],
                    start=(g == 0),
                    stop=(g == PASSES - 1),
                )
            z_of[n] = z

        def add_bias_and_measure(n):
            y = work.tile([P, C], F32, name="y", bufs=8)
            total = stats.tile([P, 1], F32, name="total")
            nc.vector.scalar_tensor_tensor(
                out=y[:],
                in0=z_of[n][:],
                scalar=1.0,
                in1=bias_all[:].rearrange("p t q -> p (t q)"),
                op0=ALU.mult,
                op1=ALU.add,
                accum_out=total[:],
            )
            neg_mean = stats.tile([P, 1], F32, name="neg_mean")
            nc.scalar.activation(out=neg_mean[:], in_=total[:], func=ACT.Copy, scale=-1.0 / C)
            unread = work.tile([P, C], BF16, name="unread", bufs=2)
            squares = stats.tile([P, 1], F32, name="squares")
            nc.scalar.activation(
                out=unread[:], in_=y[:], func=ACT.Square, bias=total[:], scale=-1.0 * C, accum_out=squares[:]
            )
            y_of[n], neg_mean_of[n], squares_of[n] = y, neg_mean, squares

        def invert_deviation(n):
            rstd = stats.tile([P, 1], F32, name="rstd")
            nc.scalar.activation(
                out=rstd[:], in_=squares_of[n][:], func=ACT.Abs_reciprocal_sqrt, bias=EPS, scale=1.0 / (C * C * C)
            )
            rstd_of[n] = rstd

        def normalise(n):
            yn = work.tile([P, C], F32, name="yn", bufs=ALL_TILES)
            if n % 2 == 0 or True:
                nc.gpsimd.tensor_scalar(
                    out=yn[:],
                    in0=y_of[n][:],
                    scalar1=neg_mean_of[n][:],
                    scalar2=rstd_of[n][:],
                    op0=ALU.add,
                    op1=ALU.mult,
                )
            else:
                shift = stats.tile([P, 1], F32, name="shift")
                nc.gpsimd.tensor_scalar(
                    out=shift[:], in0=neg_mean_of[n][:], scalar1=rstd_of[n][:], scalar2=0.0, op0=ALU.mult, op1=ALU.add
                )
                nc.scalar.activation(out=yn[:], in_=y_of[n][:], func=ACT.Identity, bias=shift[:], scale=rstd_of[n][:])
            normed_of[n] = yn

        def measure(n):
            if n < ALL_TILES:
                add_bias_and_measure(n)
            if 0 <= n - 1 < ALL_TILES:
                invert_deviation(n - 1)
            if 0 <= n - 2 < ALL_TILES:
                normalise(n - 2)

        turned_of = {}

        def turn(group):
            for t in range(C_TILES):
                turned = psum.tile([P, GROUP], F32, tag="bank")
                for i in range(TILES):
                    nc.tensor.transpose(
                        turned[:, i * P : (i + 1) * P],
                        normed_of[group * TILES + i][:, t * P : (t + 1) * P],
                        ident[:],
                    )
                turned_of[(group, t)] = turned

        helped_of = {}

        def place(group):
            b, first = group * GROUP // N, group * GROUP % N
            return b, slice(first, first + GROUP)

        def store_helped(group):
            b, cols = place(group)
            nc.scalar.dma_start(out=out_rows[b, :, HELPED, cols], in_=helped_of[group][:])

        def finish(group):
            b, cols = place(group)
            helped_here = group in HELPED_GROUPS
            for t in [t for t in range(C_TILES) if not (helped_here and t == HELPED)]:
                result = work.tile([P, GROUP], F32, name="result", bufs=10)
                nc.vector.scalar_tensor_tensor(
                    out=result[:],
                    in0=turned_of[(group, t)][:],
                    scalar=gain[:, t : t + 1],
                    in1=xn_sb[b][:, t, cols],
                    op0=ALU.mult,
                    op1=ALU.add,
                )
                nc.sync.dma_start(out=out_rows[b, :, t, cols], in_=result[:])
            if helped_here:
                scaled = work.tile([P, GROUP], F32, name="scaled", bufs=2)
                nc.scalar.activation(
                    out=scaled[:], in_=turned_of[(group, HELPED)][:], func=ACT.Copy, scale=gain[:, HELPED : HELPED + 1]
                )
                helped = work.tile([P, GROUP], F32, name="helped", bufs=2)
                nc.gpsimd.tensor_tensor(out=helped[:], in0=scaled[:], in1=xn_sb[b][:, HELPED, cols], op=ALU.add)
                helped_of[group] = helped
            if group - 1 in HELPED_GROUPS:
                store_helped(group - 1)

        for c in range(CHUNKS):
            regroup(c)
            if c > 0:
                quantise(c - 1, 1)
            quantise(c, 0)
            if 2 <= c <= PASSES + 1:
                w_quantise(c - 2)
            if 1 <= c < PASSES + 1:
                w_turn(c - 1)
            if c == PASSES + 1:
                spread_bias()
        for n in range(2 * TILES):
            project(n)
        for n in range(TILES):
            measure(n)
        quantise(CHUNKS - 1, 1)
        for n in range(2 * TILES, 3 * TILES):
            project(n)
        for n in range(TILES, 3 * TILES):
            measure(n)
        turn(0)
        for n in range(3 * TILES, ALL_TILES):
            project(n)
        finish(0)
        for n in range(3 * TILES, ALL_TILES + 2):
            measure(n)
        for group in range(1, GROUPS):
            turn(group)
            finish(group)
